import numpy as np
import ml_dtypes


def mxq(x, axis, fmt="e4m3"):
    dtype, down = {"e4m3": (ml_dtypes.float8_e4m3fn, 7), "e5m2": (ml_dtypes.float8_e5m2, 14)}[fmt]
    v = np.moveaxis(np.asarray(x, np.float32).astype(ml_dtypes.bfloat16).astype(np.float64), axis, -1)
    blocks = v.reshape(v.shape[:-1] + (-1, 32))
    amax = np.abs(blocks).max(-1, keepdims=True)
    byte = np.maximum(np.where(amax > 0, np.frexp(amax)[1] - 1 + 127, 0) - down, 1)
    scale = np.exp2(byte - 127.0)
    codes = (blocks / scale).astype(np.float32).astype(dtype).astype(np.float64)
    return np.moveaxis((codes * scale).reshape(v.shape), -1, axis)


WIDE = False


def mx_kscale(k):
    if not WIDE:
        return np.ones(k)
    levels = np.array([10, -10, 5, -5, 0])
    a = np.random.permutation(np.resize(levels, k // 512 * 4)).reshape(k // 512, 4)
    idx = np.arange(k)
    return np.exp2(a[idx // 512, idx % 128 // 32])


BF16 = ml_dtypes.bfloat16


def bf(x):
    return np.asarray(x, np.float32).astype(BF16)


def f64(x):
    return np.asarray(x).astype(np.float64)


E2M1 = np.array([0.0, 0.5, 1.0, 1.5, 2.0, 3.0, 4.0, 6.0, -0.0, -0.5, -1.0, -1.5, -2.0, -3.0, -4.0, -6.0])


def pack_weight(w, fmt):
    k, n = w.shape
    w = f64(bf(w)).reshape(k // 32, 32, n)
    amax = np.abs(w).max(1)
    if fmt == "e4m3":
        byte = np.frexp(amax)[1] - 1 + 127 - 7
    else:
        mant, ex = np.frexp(amax / 6.0)
        byte = np.where(mant > 0.5, ex, ex - 1) + 127
    byte = np.clip(np.where(amax > 0, byte, 1), 1, 254)
    scaled = (w * np.exp2(127.0 - byte)[:, None, :]).reshape(k, n).astype(np.float32)
    by_word = np.ascontiguousarray(scaled.reshape(k // 512, 128, 4, n).transpose(0, 1, 3, 2))
    if fmt == "e4m3":
        words = by_word.astype(ml_dtypes.float8_e4m3fn).view(np.uint8)
    else:
        c = by_word.astype(ml_dtypes.float4_e2m1fn).view(np.uint8) & 0xF
        words = c[..., 0::2] | (c[..., 1::2] << 4)
    return np.ascontiguousarray(words), np.ascontiguousarray(byte.astype(np.uint8).reshape(k // 512, 16, n))


def unpack_weight(words, scales, fmt):
    g, p, n, _ = words.shape
    if fmt == "e4m3":
        vals = np.ascontiguousarray(words).view(ml_dtypes.float8_e4m3fn).astype(np.float64)
    else:
        nib = np.empty((g, p, n, 4), np.uint8)
        nib[..., 0::2] = words & 0xF
        nib[..., 1::2] = words >> 4
        vals = E2M1[nib]
    vals = vals * np.repeat(np.exp2(scales.astype(np.float64) - 127.0), 8, axis=1)[..., None]
    return vals.transpose(0, 1, 3, 2).reshape(g * 512, n)

def pack4(w):
    words, scales = pack_weight(w, "e2m1")
    return words.reshape(words.shape[0], 128, -1), scales


def unpack4(words, scales):
    return unpack_weight(words.reshape(words.shape[0], 128, -1, 2), scales, "e2m1")


B, IDIM, HDIM, ODIM, S, DEPTH, NACT, NTOP = 512, 8192, 1024, 512, 128, 32, 3, 2


def sigmoid(v):
    return 1.0 / (1.0 + np.exp(-v))


def setup_inputs():
    s, t = mx_kscale(IDIM), mx_kscale(HDIM)
    x = bf(np.random.standard_normal((B, IDIM)) * s)
    hidden = bf(np.random.standard_normal((B, HDIM)) * t)
    stack_top = bf(np.random.standard_normal((B, NTOP, S)))
    Wi = np.random.standard_normal((HDIM, IDIM)) * 0.7 / np.sqrt(IDIM) / s
    bi = bf(np.random.standard_normal(HDIM) * 0.2)
    Wh = np.random.standard_normal((HDIM, HDIM)) * 0.7 / np.sqrt(HDIM) / t
    bh = bf(np.random.standard_normal(HDIM) * 0.2)
    W0 = bf(np.random.standard_normal((HDIM, S)) * 0.5 / np.sqrt(S))
    b0 = bf(np.random.standard_normal(HDIM) * 0.2)
    W1 = bf(np.random.standard_normal((HDIM, S)) * 0.5 / np.sqrt(S))
    b1 = bf(np.random.standard_normal(HDIM) * 0.2)
    Wi_words, Wi_scales = pack4(np.ascontiguousarray(Wi.T))
    Wh_words, Wh_scales = pack4(np.ascontiguousarray(Wh.T))
    return {"x": x,
            "hidden": hidden,
            "stack_top": stack_top,
            "Wi_words": Wi_words,
            "Wi_scales": Wi_scales,
            "bi": bi,
            "Wh_words": Wh_words,
            "Wh_scales": Wh_scales,
            "bh": bh,
            "W0": W0,
            "b0": b0,
            "W1": W1,
            "b1": b1}


def reference(x, hidden, stack_top, Wi_words, Wi_scales, bi, Wh_words, Wh_scales, bh, W0, b0, W1, b1):
    pre = ((mxq(f64(x), 1, "e4m3") @ unpack4(Wi_words, Wi_scales)) + f64(bi)
           + (mxq(f64(hidden), 1, "e4m3") @ unpack4(Wh_words, Wh_scales)) + f64(bh)
           + f64(stack_top)[:, 0] @ f64(W0).T + f64(b0)
           + f64(stack_top)[:, 1] @ f64(W1).T + f64(b1))
    return sigmoid(pre)

@@ -1,0 +1,225 @@
+from contextlib import ExitStack
+
+import concourse.mybir as mybir
+from concourse.masks import make_identity
+
+F32 = mybir.dt.float32
+BF16 = mybir.dt.bfloat16
+I32 = mybir.dt.int32
+U32 = mybir.dt.uint32
+U8 = mybir.dt.uint8
+FP8X4 = mybir.dt.float8_e4m3fn_x4
+FP4X4 = mybir.dt.float4_e2m1fn_x4
+
+P = 128
+PACK = 4
+K_PASS = P * PACK
+PAIRS = 2
+
+BATCH, IDIM, HDIM, SDIM = 512, 8192, 1024, 128
+BATCH_TILES = BATCH // P
+ROUND_TILES = 2
+ROUNDS = BATCH_TILES // ROUND_TILES
+N_HALF = 512
+N_HALVES = HDIM // N_HALF
+CHUNK_PASSES = 4
+SCALE_ROWS = K_PASS // 32
+
+FLOPS = 2 * BATCH * HDIM * (IDIM + HDIM + 2 * SDIM)
+
+
+def tile_stackrnn_pa_k_kernel(
+    tc, x, hidden, stack_top, Wi_words, Wi_scales, bi, Wh_words, Wh_scales, bh, W0, b0, W1, b1, out
+):
+    nc = tc.nc
+
+    chunks = []
+    for source, k_size in (("x", IDIM), ("hidden", HDIM)):
+        source_passes = k_size // K_PASS
+        for first in range(0, source_passes, CHUNK_PASSES):
+            chunks.append((source, first, min(CHUNK_PASSES, source_passes - first)))
+    steps = [(r, c) for r in range(ROUNDS) for c in range(len(chunks))]
+
+    activations = {
+        "x": x.rearrange("(p t) k -> p t k", t=BATCH_TILES),
+        "hidden": hidden.rearrange("(p t) k -> p t k", t=BATCH_TILES),
+    }
+    word_rows = {
+        "x": Wi_words.bitcast(I32).rearrange("g p m -> p g m"),
+        "hidden": Wh_words.bitcast(I32).rearrange("g p m -> p g m"),
+    }
+    scale_rows = {
+        "x": Wi_scales.bitcast(I32).rearrange("g (h i) n -> i h g n", h=2),
+        "hidden": Wh_scales.bitcast(I32).rearrange("g (h i) n -> i h g n", h=2),
+    }
+    out_rows = out.rearrange("(p t) n -> p t n", t=BATCH_TILES)
+
+    with ExitStack() as ctx:
+        keep = ctx.enter_context(tc.tile_pool(name="keep", bufs=1))
+        stage = ctx.enter_context(tc.tile_pool(name="stage", bufs=2))
+        sums_pool = ctx.enter_context(tc.psum_pool(name="sums_pool", bufs=ROUND_TILES * N_HALVES))
+        work = ctx.enter_context(tc.psum_pool(name="work", bufs=4))
+        ctx.enter_context(tc.manual_schedule())
+
+        ident_bf16 = keep.tile([P, P], BF16)
+        make_identity(nc, ident_bf16[:])
+        ident_f32 = keep.tile([P, P], F32)
+        make_identity(nc, ident_f32[:])
+        ones = keep.tile([P, P], BF16)
+        nc.vector.memset(ones[:], 1.0)
+        bias_rows = keep.tile([P, HDIM], BF16)
+        nc.vector.memset(bias_rows[:], 0.0)
+        w_words = []
+        w_planes = []
+        for c in range(len(chunks)):
+            passes = chunks[c][2]
+            w_words.append(keep.tile([P, passes, 2 * HDIM], U8, name="w_words_%d" % c, align_bytes=64))
+            w_planes.append(keep.tile([P, passes, HDIM], U8, name="w_planes_%d" % c, align_bytes=64))
+            nc.vector.memset(w_planes[c][:].bitcast(I32), 0)
+
+        for row, bias in enumerate((bi, bh, b0, b1)):
+            nc.scalar.dma_start(out=bias_rows[row : row + 1, :], in_=bias.rearrange("(o n) -> o n", o=1))
+        st_raw = keep.tile([P, BATCH_TILES, 2, SDIM], BF16)
+        nc.sync.dma_start(out=st_raw[:], in_=stack_top.rearrange("(p t) j s -> p t j s", t=BATCH_TILES))
+        ws_raw = []
+        for j, w_stack in enumerate((W0, W1)):
+            ws_raw.append(keep.tile([P, HDIM // P, SDIM], BF16, name="ws_raw_%d" % j))
+            nc.sync.dma_start(out=ws_raw[j][:], in_=w_stack.rearrange("(c p) s -> p c s", p=P))
+
+        raw_tiles = {}
+
+        def load_activations(step):
+            r, c = steps[step]
+            source, first, passes = chunks[c]
+            raw = keep.tile([P, ROUND_TILES, passes * K_PASS], BF16, name="raw_%d_%d" % (r, c))
+            nc.sync.dma_start(
+                out=raw[:],
+                in_=activations[source][
+                    :, r * ROUND_TILES : (r + 1) * ROUND_TILES, first * K_PASS : (first + passes) * K_PASS
+                ],
+            )
+            raw_tiles[step] = raw
+
+        def load_weights(c):
+            source, first, passes = chunks[c]
+            for i in range(SCALE_ROWS // 2):
+                partition = 32 * (i // 4) + i % 4
+                nc.sync.dma_start(
+                    out=w_planes[c][partition:P:64, :, :].bitcast(I32),
+                    in_=scale_rows[source][i, :, first : first + passes, :],
+                )
+            nc.sync.dma_start(out=w_words[c][:].bitcast(I32), in_=word_rows[source][:, first : first + passes, :])
+
+        load_activations(0)
+        load_activations(1)
+        for step in range(len(steps)):
+            if step < len(chunks):
+                load_weights(step)
+            if step + 2 < len(steps):
+                load_activations(step + 2)
+
+        st_flipped = work.tile([P, 2, BATCH_TILES, P], BF16, tag="work")
+        for j in range(2):
+            for t in range(BATCH_TILES):
+                nc.tensor.transpose(st_flipped[:, j, t, :], st_raw[:, t, j, :], ident_bf16[:])
+        st_T = keep.tile([P, 2, BATCH_TILES, P], BF16)
+        nc.scalar.copy(out=st_T[:], in_=st_flipped[:])
+        ws_T = []
+        for j in range(2):
+            ws_flipped = work.tile([P, HDIM], BF16, tag="work")
+            for c in range(HDIM // P):
+                nc.tensor.transpose(ws_flipped[:, c * P : (c + 1) * P], ws_raw[j][:, c, :], ident_bf16[:])
+            ws_T.append(keep.tile([P, HDIM], BF16, name="ws_T_%d" % j))
+            nc.scalar.copy(out=ws_T[j][:], in_=ws_flipped[:])
+        pre_act = []
+        for tile_index in range(BATCH_TILES):
+            pre_act.append(keep.tile([P, HDIM], F32, name="pre_act_%d" % tile_index))
+            for h in range(N_HALVES):
+                n_cols = slice(h * N_HALF, (h + 1) * N_HALF)
+                plain = work.tile([P, N_HALF], F32, tag="work")
+                for j in range(2):
+                    nc.tensor.matmul(
+                        out=plain[:], lhsT=st_T[:, j, tile_index, :], rhs=ws_T[j][:, n_cols], start=(j == 0), stop=False
+                    )
+                nc.tensor.matmul(out=plain[:], lhsT=ones[:], rhs=bias_rows[:, n_cols], start=False, stop=True)
+                nc.scalar.copy(out=pre_act[tile_index][:, n_cols], in_=plain[:])
+
+        sorted_tiles = {}
+        grouped_tiles = {}
+        code_tiles = {}
+        sums = {}
+
+        def sort_pairs(step):
+            passes = chunks[steps[step][1]][2]
+            sorted_pairs = stage.tile([P, ROUND_TILES, passes, PAIRS, P], F32, name="sorted_pairs")
+            nc.vector.tensor_copy(
+                out=sorted_pairs[:],
+                in_=raw_tiles[step][:].bitcast(F32).rearrange("p t (g q u) -> p t g u q", q=P, u=PAIRS),
+            )
+            sorted_tiles[step] = sorted_pairs
+
+        def flip(step):
+            passes = chunks[steps[step][1]][2]
+            grouped = stage.tile([P, passes * ROUND_TILES * P * PACK], BF16, name="grouped", align_bytes=64)
+            grouped_pairs = grouped[:].bitcast(F32).rearrange(
+                "q (g t b u) -> q g t b u", g=passes, t=ROUND_TILES, u=PAIRS
+            )
+            for g in range(passes):
+                flipped = work.tile([P, ROUND_TILES, PAIRS, P], F32, tag="work")
+                for t in range(ROUND_TILES):
+                    for u in range(PAIRS):
+                        nc.tensor.transpose(flipped[:, t, u, :], sorted_tiles[step][:, t, g, u, :], ident_f32[:])
+                nc.scalar.copy(out=grouped_pairs[:, g], in_=flipped[:].rearrange("q t u b -> q t b u"))
+            grouped_tiles[step] = grouped
+
+        def quantise(step):
+            passes = chunks[steps[step][1]][2]
+            codes = stage.tile([P, passes * ROUND_TILES * P], U32, name="codes", align_bytes=64)
+            x_planes = stage.tile([P, passes * ROUND_TILES * P], U8, name="x_planes", align_bytes=64)
+            nc.vector.quantize_mx(out=codes[:].bitcast(FP8X4), scales=x_planes[:], in_=grouped_tiles[step][:])
+            code_tiles[step] = (codes, x_planes)
+
+        def multiply(step):
+            c = steps[step][1]
+            passes = chunks[c][2]
+            codes, x_planes = code_tiles[step]
+            for t in range(ROUND_TILES):
+                for h in range(N_HALVES):
+                    if c == 0:
+                        sums[(t, h)] = sums_pool.tile([P, N_HALF], F32, name="sums")
+                    for g in range(passes):
+                        b_cols = slice((g * ROUND_TILES + t) * P, (g * ROUND_TILES + t + 1) * P)
+                        nc.tensor.matmul_mx(
+                            out=sums[(t, h)][:],
+                            lhsT=codes[:, b_cols].bitcast(FP8X4),
+                            lhsT_scale=x_planes[:, b_cols],
+                            rhs=w_words[c][:, g, 2 * h * N_HALF : 2 * (h + 1) * N_HALF].bitcast(FP4X4),
+                            rhs_scale=w_planes[c][:, g, h * N_HALF : (h + 1) * N_HALF],
+                            start=(c == 0 and g == 0),
+                            stop=(c == len(chunks) - 1 and g == passes - 1),
+                        )
+
+        def finish(r):
+            for t in range(ROUND_TILES):
+                for h in range(N_HALVES):
+                    tile_index = r * ROUND_TILES + t
+                    n_cols = slice(h * N_HALF, (h + 1) * N_HALF)
+                    part = pre_act[tile_index][:, n_cols]
+                    nc.vector.tensor_tensor(out=part, in0=sums[(t, h)][:], in1=part, op=mybir.AluOpType.add)
+                    nc.scalar.activation(out=part, in_=part, func=mybir.ActivationFunctionType.Sigmoid)
+                    nc.sync.dma_start(out=out_rows[:, tile_index, n_cols], in_=part)
+
+        sort_pairs(0)
+        flip(0)
+        sort_pairs(1)
+        for step in range(len(steps)):
+            quantise(step)
+            if step + 1 < len(steps):
+                flip(step + 1)
+            if step + 2 < len(steps):
+                sort_pairs(step + 2)
+            r, c = steps[step]
+            if c == 0 and r > 0:
+                finish(r - 1)
+            multiply(step)
+        finish(ROUNDS - 1)

@@ -69,13 +69,10 @@ def tile_stackrnn_pa_k_kernel(
         nc.vector.memset(ones[:], 1.0)
         bias_rows = keep.tile([P, HDIM], BF16)
         nc.vector.memset(bias_rows[:], 0.0)
-        w_words = []
-        w_planes = []
-        for c in range(len(chunks)):
-            passes = chunks[c][2]
-            w_words.append(keep.tile([P, passes, 2 * HDIM], U8, name="w_words_%d" % c, align_bytes=64))
-            w_planes.append(keep.tile([P, passes, HDIM], U8, name="w_planes_%d" % c, align_bytes=64))
-            nc.vector.memset(w_planes[c][:].bitcast(I32), 0)
+        w_planes = {}
+        for source, k_size in (("x", IDIM), ("hidden", HDIM)):
+            w_planes[source] = keep.tile([P, k_size // K_PASS, HDIM], U8, name="w_planes_" + source, align_bytes=64)
+            nc.vector.memset(w_planes[source][:].bitcast(I32), 0)
 
         for row, bias in enumerate((bi, bh, b0, b1)):
             nc.scalar.dma_start(out=bias_rows[row : row + 1, :], in_=bias.rearrange("(o n) -> o n", o=1))
@@ -100,14 +97,15 @@ def tile_stackrnn_pa_k_kernel(
             )
             raw_tiles[step] = raw
 
+        w_words = []
+
         def load_weights(c):
             source, first, passes = chunks[c]
-            for i in range(SCALE_ROWS // 2):
-                partition = 32 * (i // 4) + i % 4
-                nc.sync.dma_start(
-                    out=w_planes[c][partition:P:64, :, :].bitcast(I32),
-                    in_=scale_rows[source][i, :, first : first + passes, :],
-                )
+            if first == 0:
+                for i in range(SCALE_ROWS // 2):
+                    partition = 32 * (i // 4) + i % 4
+                    nc.sync.dma_start(out=w_planes[source][partition:P:64, :, :].bitcast(I32), in_=scale_rows[source][i])
+            w_words.append(keep.tile([P, passes, 2 * HDIM], U8, name="w_words_%d" % c, align_bytes=64))
             nc.sync.dma_start(out=w_words[c][:].bitcast(I32), in_=word_rows[source][:, first : first + passes, :])
 
         load_activations(0)
@@ -139,10 +137,16 @@ def tile_stackrnn_pa_k_kernel(
                 plain = work.tile([P, N_HALF], F32, tag="work")
                 for j in range(2):
                     nc.tensor.matmul(
-                        out=plain[:], lhsT=st_T[:, j, tile_index, :], rhs=ws_T[j][:, n_cols], start=(j == 0), stop=False
+                        out=plain[:], lhsT=st_T[:, j, tile_index, :], rhs=ws_T[j][:, n_cols], start=(j == 0), stop=(j == 1)
                     )
-                nc.tensor.matmul(out=plain[:], lhsT=ones[:], rhs=bias_rows[:, n_cols], start=False, stop=True)
                 nc.scalar.copy(out=pre_act[tile_index][:, n_cols], in_=plain[:])
+
+        bias_all = keep.tile([P, HDIM], F32)
+        for h in range(N_HALVES):
+            n_cols = slice(h * N_HALF, (h + 1) * N_HALF)
+            spread = work.tile([P, N_HALF], F32, tag="work")
+            nc.tensor.matmul(out=spread[:], lhsT=ones[:], rhs=bias_rows[:, n_cols], start=True, stop=True)
+            nc.scalar.copy(out=bias_all[:, n_cols], in_=spread[:])
 
         sorted_tiles = {}
         grouped_tiles = {}
@@ -181,7 +185,7 @@ def tile_stackrnn_pa_k_kernel(
 
         def multiply(step):
             c = steps[step][1]
-            passes = chunks[c][2]
+            source, first, passes = chunks[c]
             codes, x_planes = code_tiles[step]
             for t in range(ROUND_TILES):
                 for h in range(N_HALVES):
@@ -194,7 +198,7 @@ def tile_stackrnn_pa_k_kernel(
                             lhsT=codes[:, b_cols].bitcast(FP8X4),
                             lhsT_scale=x_planes[:, b_cols],
                             rhs=w_words[c][:, g, 2 * h * N_HALF : 2 * (h + 1) * N_HALF].bitcast(FP4X4),
-                            rhs_scale=w_planes[c][:, g, h * N_HALF : (h + 1) * N_HALF],
+                            rhs_scale=w_planes[source][:, first + g, h * N_HALF : (h + 1) * N_HALF],
                             start=(c == 0 and g == 0),
                             stop=(c == len(chunks) - 1 and g == passes - 1),
                         )
@@ -218,6 +222,10 @@ def tile_stackrnn_pa_k_kernel(
                 flip(step + 1)
             if step + 2 < len(steps):
                 sort_pairs(step + 2)
+            if step < BATCH_TILES:
+                nc.vector.tensor_tensor(
+                    out=pre_act[step][:], in0=pre_act[step][:], in1=bias_all[:], op=mybir.AluOpType.add
+                )
             r, c = steps[step]
             if c == 0 and r > 0:
                 finish(r - 1)

@@ -18,12 +18,14 @@ PAIRS = 2
 
 BATCH, IDIM, HDIM, SDIM = 512, 8192, 1024, 128
 BATCH_TILES = BATCH // P
-ROUND_TILES = 2
-ROUNDS = BATCH_TILES // ROUND_TILES
 N_HALF = 512
 N_HALVES = HDIM // N_HALF
-CHUNK_PASSES = 4
+STEP_PASSES = 2
 SCALE_ROWS = K_PASS // 32
+RAW_BUFS = 6
+ROUND1_STEPS = 3
+
+assert (IDIM + HDIM) // (K_PASS * STEP_PASSES) % ROUND1_STEPS == 0
 
 FLOPS = 2 * BATCH * HDIM * (IDIM + HDIM + 2 * SDIM)
 
@@ -33,12 +35,11 @@ def tile_stackrnn_pa_k_kernel(
 ):
     nc = tc.nc
 
-    chunks = []
-    for source, k_size in (("x", IDIM), ("hidden", HDIM)):
-        source_passes = k_size // K_PASS
-        for first in range(0, source_passes, CHUNK_PASSES):
-            chunks.append((source, first, min(CHUNK_PASSES, source_passes - first)))
-    steps = [(r, c) for r in range(ROUNDS) for c in range(len(chunks))]
+    k_sizes = {"x": IDIM, "hidden": HDIM}
+    steps = []
+    for source in ("x", "hidden"):
+        for first in range(0, k_sizes[source] // K_PASS, STEP_PASSES):
+            steps.append((source, first))
 
     activations = {
         "x": x.rearrange("(p t) k -> p t k", t=BATCH_TILES),
@@ -49,104 +50,122 @@ def tile_stackrnn_pa_k_kernel(
         "hidden": Wh_words.bitcast(I32).rearrange("g p m -> p g m"),
     }
     scale_rows = {
-        "x": Wi_scales.bitcast(I32).rearrange("g (h i) n -> i h g n", h=2),
-        "hidden": Wh_scales.bitcast(I32).rearrange("g (h i) n -> i h g n", h=2),
+        "x": Wi_scales.bitcast(I32).rearrange("g (two i) n -> i two g n", two=2),
+        "hidden": Wh_scales.bitcast(I32).rearrange("g (two i) n -> i two g n", two=2),
     }
     out_rows = out.rearrange("(p t) n -> p t n", t=BATCH_TILES)
 
     with ExitStack() as ctx:
         keep = ctx.enter_context(tc.tile_pool(name="keep", bufs=1))
+        raw_pool = ctx.enter_context(tc.tile_pool(name="raw_pool", bufs=RAW_BUFS))
         stage = ctx.enter_context(tc.tile_pool(name="stage", bufs=2))
-        sums_pool = ctx.enter_context(tc.psum_pool(name="sums_pool", bufs=ROUND_TILES * N_HALVES))
+        sums_pool = ctx.enter_context(tc.psum_pool(name="sums_pool", bufs=BATCH_TILES))
         work = ctx.enter_context(tc.psum_pool(name="work", bufs=4))
         ctx.enter_context(tc.manual_schedule())
 
-        ident_bf16 = keep.tile([P, P], BF16)
-        make_identity(nc, ident_bf16[:])
-        ident_f32 = keep.tile([P, P], F32)
-        make_identity(nc, ident_f32[:])
+        ident = keep.tile([P, P], F32)
+        make_identity(nc, ident[:])
         ones = keep.tile([P, P], BF16)
         nc.vector.memset(ones[:], 1.0)
         bias_rows = keep.tile([P, HDIM], BF16)
         nc.vector.memset(bias_rows[:], 0.0)
         w_planes = {}
-        for source, k_size in (("x", IDIM), ("hidden", HDIM)):
-            w_planes[source] = keep.tile([P, k_size // K_PASS, HDIM], U8, name="w_planes_" + source, align_bytes=64)
-            nc.vector.memset(w_planes[source][:].bitcast(I32), 0)
-
-        for row, bias in enumerate((bi, bh, b0, b1)):
-            nc.scalar.dma_start(out=bias_rows[row : row + 1, :], in_=bias.rearrange("(o n) -> o n", o=1))
-        st_raw = keep.tile([P, BATCH_TILES, 2, SDIM], BF16)
-        nc.sync.dma_start(out=st_raw[:], in_=stack_top.rearrange("(p t) j s -> p t j s", t=BATCH_TILES))
-        ws_raw = []
-        for j, w_stack in enumerate((W0, W1)):
-            ws_raw.append(keep.tile([P, HDIM // P, SDIM], BF16, name="ws_raw_%d" % j))
-            nc.sync.dma_start(out=ws_raw[j][:], in_=w_stack.rearrange("(c p) s -> p c s", p=P))
+        for h in range(N_HALVES):
+            for source in ("x", "hidden"):
+                w_planes[(source, h)] = keep.tile(
+                    [P, k_sizes[source] // K_PASS, N_HALF], U8, name="w_planes_%s_%d" % (source, h), align_bytes=64
+                )
+                nc.vector.memset(w_planes[(source, h)][:].bitcast(I32), 0)
 
         raw_tiles = {}
+        w_words = {}
 
         def load_activations(step):
-            r, c = steps[step]
-            source, first, passes = chunks[c]
-            raw = keep.tile([P, ROUND_TILES, passes * K_PASS], BF16, name="raw_%d_%d" % (r, c))
+            source, first = steps[step]
+            raw = raw_pool.tile([P, BATCH_TILES, STEP_PASSES * K_PASS], BF16, name="raw")
             nc.sync.dma_start(
-                out=raw[:],
-                in_=activations[source][
-                    :, r * ROUND_TILES : (r + 1) * ROUND_TILES, first * K_PASS : (first + passes) * K_PASS
-                ],
+                out=raw[:], in_=activations[source][:, :, first * K_PASS : (first + STEP_PASSES) * K_PASS]
             )
             raw_tiles[step] = raw
 
-        w_words = []
-
-        def load_weights(c):
-            source, first, passes = chunks[c]
+        def load_weights(step, h):
+            source, first = steps[step]
             if first == 0:
                 for i in range(SCALE_ROWS // 2):
                     partition = 32 * (i // 4) + i % 4
-                    nc.sync.dma_start(out=w_planes[source][partition:P:64, :, :].bitcast(I32), in_=scale_rows[source][i])
-            w_words.append(keep.tile([P, passes, 2 * HDIM], U8, name="w_words_%d" % c, align_bytes=64))
-            nc.sync.dma_start(out=w_words[c][:].bitcast(I32), in_=word_rows[source][:, first : first + passes, :])
+                    nc.sync.dma_start(
+                        out=w_planes[(source, h)][partition:P:64, :, :].bitcast(I32),
+                        in_=scale_rows[source][i, :, :, h * N_HALF // 4 : (h + 1) * N_HALF // 4],
+                    )
+            words = keep.tile([P, STEP_PASSES, 2 * N_HALF], U8, name="w_words_%d_%d" % (h, step), align_bytes=64)
+            nc.sync.dma_start(
+                out=words[:].bitcast(I32),
+                in_=word_rows[source][:, first : first + STEP_PASSES, h * N_HALF // 2 : (h + 1) * N_HALF // 2],
+            )
+            w_words[(h, step)] = words
 
-        load_activations(0)
-        load_activations(1)
-        for step in range(len(steps)):
-            if step < len(chunks):
-                load_weights(step)
-            if step + 2 < len(steps):
-                load_activations(step + 2)
+        def fetch(k):
+            if 0 <= k - 2 < len(steps):
+                load_weights(k - 2, 0)
+            if k < len(steps):
+                load_activations(k)
 
-        st_flipped = work.tile([P, 2, BATCH_TILES, P], BF16, tag="work")
-        for j in range(2):
-            for t in range(BATCH_TILES):
-                nc.tensor.transpose(st_flipped[:, j, t, :], st_raw[:, t, j, :], ident_bf16[:])
-        st_T = keep.tile([P, 2, BATCH_TILES, P], BF16)
-        nc.scalar.copy(out=st_T[:], in_=st_flipped[:])
+        st_raw = keep.tile([P, BATCH_TILES, 2 * SDIM], BF16)
+        nc.sync.dma_start(out=st_raw[:], in_=stack_top.rearrange("(p t) j s -> p t (j s)", t=BATCH_TILES))
+        ws_raw = keep.tile([P, HDIM // P, 2, SDIM], BF16)
+        for j, w_stack in enumerate((W0, W1)):
+            nc.sync.dma_start(out=ws_raw[:, :, j, :], in_=w_stack.rearrange("(c p) s -> p c s", p=P))
+        for k in range(RAW_BUFS):
+            fetch(k)
+        for row, bias in enumerate((bi, bh, b0, b1)):
+            nc.sync.dma_start(out=bias_rows[row : row + 1, :], in_=bias.rearrange("(o n) -> o n", o=1))
+
+        st_flipped = work.tile([P, BATCH_TILES, P], F32, tag="work")
+        for t in range(BATCH_TILES):
+            nc.tensor.transpose(st_flipped[:, t, :], st_raw[:, t, :].bitcast(F32), ident[:])
+        st_T = keep.tile([P, BATCH_TILES, P, 2], BF16)
+        nc.vector.tensor_copy(
+            out=st_T[:].rearrange("q t b e -> q (t b e)"),
+            in_=st_flipped[:].rearrange("q t b -> q (t b)").bitcast(BF16),
+        )
         ws_T = []
-        for j in range(2):
-            ws_flipped = work.tile([P, HDIM], BF16, tag="work")
-            for c in range(HDIM // P):
-                nc.tensor.transpose(ws_flipped[:, c * P : (c + 1) * P], ws_raw[j][:, c, :], ident_bf16[:])
-            ws_T.append(keep.tile([P, HDIM], BF16, name="ws_T_%d" % j))
-            nc.scalar.copy(out=ws_T[j][:], in_=ws_flipped[:])
+        blocks = N_HALF // P
+        for h in range(N_HALVES):
+            ws_flipped = work.tile([P, blocks, P], F32, tag="work")
+            for c in range(blocks):
+                nc.tensor.transpose(
+                    ws_flipped[:, c, :],
+                    ws_raw[:, h * blocks + c, :, :].rearrange("p j s -> p (j s)").bitcast(F32),
+                    ident[:],
+                )
+            ws_T.append(keep.tile([P, N_HALF, 2], BF16, name="ws_T_%d" % h))
+            nc.scalar.copy(
+                out=ws_T[h][:].rearrange("q n e -> q (n e)"),
+                in_=ws_flipped[:].rearrange("q c n -> q (c n)").bitcast(BF16),
+            )
+
         pre_act = []
-        for tile_index in range(BATCH_TILES):
-            pre_act.append(keep.tile([P, HDIM], F32, name="pre_act_%d" % tile_index))
+        for t in range(BATCH_TILES):
+            pre_act.append(keep.tile([P, HDIM], F32, name="pre_act_%d" % t))
+
+        def plain_products(h):
+            for t in range(BATCH_TILES):
+                plain = sums_pool.tile([P, N_HALF], F32, tag="sums")
+                for e in range(2):
+                    nc.tensor.matmul(
+                        out=plain[:], lhsT=st_T[:, t, :, e], rhs=ws_T[h][:, :, e], start=(e == 0), stop=(e == 1)
+                    )
+                nc.scalar.copy(out=pre_act[t][:, h * N_HALF : (h + 1) * N_HALF], in_=plain[:])
+
+        def add_biases():
+            bias_all = keep.tile([P, HDIM], F32)
             for h in range(N_HALVES):
                 n_cols = slice(h * N_HALF, (h + 1) * N_HALF)
-                plain = work.tile([P, N_HALF], F32, tag="work")
-                for j in range(2):
-                    nc.tensor.matmul(
-                        out=plain[:], lhsT=st_T[:, j, tile_index, :], rhs=ws_T[j][:, n_cols], start=(j == 0), stop=(j == 1)
-                    )
-                nc.scalar.copy(out=pre_act[tile_index][:, n_cols], in_=plain[:])
-
-        bias_all = keep.tile([P, HDIM], F32)
-        for h in range(N_HALVES):
-            n_cols = slice(h * N_HALF, (h + 1) * N_HALF)
-            spread = work.tile([P, N_HALF], F32, tag="work")
-            nc.tensor.matmul(out=spread[:], lhsT=ones[:], rhs=bias_rows[:, n_cols], start=True, stop=True)
-            nc.scalar.copy(out=bias_all[:, n_cols], in_=spread[:])
+                spread = work.tile([P, N_HALF], F32, tag="work")
+                nc.tensor.matmul(out=spread[:], lhsT=ones[:], rhs=bias_rows[:, n_cols], start=True, stop=True)
+                nc.scalar.copy(out=bias_all[:, n_cols], in_=spread[:])
+            for t in range(BATCH_TILES):
+                nc.vector.tensor_tensor(out=pre_act[t][:], in0=pre_act[t][:], in1=bias_all[:], op=mybir.AluOpType.add)
 
         sorted_tiles = {}
         grouped_tiles = {}
@@ -154,67 +173,67 @@ def tile_stackrnn_pa_k_kernel(
         sums = {}
 
         def sort_pairs(step):
-            passes = chunks[steps[step][1]][2]
-            sorted_pairs = stage.tile([P, ROUND_TILES, passes, PAIRS, P], F32, name="sorted_pairs")
+            sorted_pairs = stage.tile([P, BATCH_TILES, STEP_PASSES, PAIRS, P], F32, name="sorted_pairs")
             nc.vector.tensor_copy(
                 out=sorted_pairs[:],
                 in_=raw_tiles[step][:].bitcast(F32).rearrange("p t (g q u) -> p t g u q", q=P, u=PAIRS),
             )
             sorted_tiles[step] = sorted_pairs
+            fetch(step + RAW_BUFS)
 
         def flip(step):
-            passes = chunks[steps[step][1]][2]
-            grouped = stage.tile([P, passes * ROUND_TILES * P * PACK], BF16, name="grouped", align_bytes=64)
+            grouped = stage.tile([P, BATCH_TILES * STEP_PASSES * P * PACK], BF16, name="grouped", align_bytes=64)
             grouped_pairs = grouped[:].bitcast(F32).rearrange(
-                "q (g t b u) -> q g t b u", g=passes, t=ROUND_TILES, u=PAIRS
+                "q (t g b u) -> q t g b u", t=BATCH_TILES, g=STEP_PASSES, u=PAIRS
             )
-            for g in range(passes):
-                flipped = work.tile([P, ROUND_TILES, PAIRS, P], F32, tag="work")
-                for t in range(ROUND_TILES):
+            for t in range(BATCH_TILES):
+                flipped = work.tile([P, STEP_PASSES, PAIRS, P], F32, tag="work")
+                for g in range(STEP_PASSES):
                     for u in range(PAIRS):
-                        nc.tensor.transpose(flipped[:, t, u, :], sorted_tiles[step][:, t, g, u, :], ident_f32[:])
-                nc.scalar.copy(out=grouped_pairs[:, g], in_=flipped[:].rearrange("q t u b -> q t b u"))
+                        nc.tensor.transpose(flipped[:, g, u, :], sorted_tiles[step][:, t, g, u, :], ident[:])
+                nc.scalar.copy(out=grouped_pairs[:, t], in_=flipped[:].rearrange("q g u b -> q g b u"))
             grouped_tiles[step] = grouped
 
         def quantise(step):
-            passes = chunks[steps[step][1]][2]
-            codes = stage.tile([P, passes * ROUND_TILES * P], U32, name="codes", align_bytes=64)
-            x_planes = stage.tile([P, passes * ROUND_TILES * P], U8, name="x_planes", align_bytes=64)
+            codes = keep.tile([P, BATCH_TILES * STEP_PASSES * P], U32, name="codes_%d" % step, align_bytes=64)
+            x_planes = keep.tile([P, BATCH_TILES * STEP_PASSES * P], U8, name="x_planes_%d" % step, align_bytes=64)
             nc.vector.quantize_mx(out=codes[:].bitcast(FP8X4), scales=x_planes[:], in_=grouped_tiles[step][:])
             code_tiles[step] = (codes, x_planes)
 
-        def multiply(step):
-            c = steps[step][1]
-            source, first, passes = chunks[c]
-            codes, x_planes = code_tiles[step]
-            for t in range(ROUND_TILES):
-                for h in range(N_HALVES):
-                    if c == 0:
-                        sums[(t, h)] = sums_pool.tile([P, N_HALF], F32, name="sums")
-                    for g in range(passes):
-                        b_cols = slice((g * ROUND_TILES + t) * P, (g * ROUND_TILES + t + 1) * P)
+        def multiply(first_step, n_steps, h):
+            for t in range(BATCH_TILES):
+                if first_step == 0:
+                    if h == 0:
+                        sums[(h, t)] = sums_pool.tile([P, N_HALF], F32, name="sums", tag="sums")
+                    else:
+                        sums[(h, t)] = work.tile([P, N_HALF], F32, name="sums", tag="work")
+                for step in range(first_step, first_step + n_steps):
+                    source, first = steps[step]
+                    codes, x_planes = code_tiles[step]
+                    for g in range(STEP_PASSES):
+                        b_cols = slice((t * STEP_PASSES + g) * P, (t * STEP_PASSES + g + 1) * P)
                         nc.tensor.matmul_mx(
-                            out=sums[(t, h)][:],
+                            out=sums[(h, t)][:],
                             lhsT=codes[:, b_cols].bitcast(FP8X4),
                             lhsT_scale=x_planes[:, b_cols],
-                            rhs=w_words[c][:, g, 2 * h * N_HALF : 2 * (h + 1) * N_HALF].bitcast(FP4X4),
-                            rhs_scale=w_planes[source][:, first + g, h * N_HALF : (h + 1) * N_HALF],
-                            start=(c == 0 and g == 0),
-                            stop=(c == len(chunks) - 1 and g == passes - 1),
+                            rhs=w_words[(h, step)][:, g, :].bitcast(FP4X4),
+                            rhs_scale=w_planes[(source, h)][:, first + g, :],
+                            start=(step == 0 and g == 0),
+                            stop=(step == len(steps) - 1 and g == STEP_PASSES - 1),
                         )
 
-        def finish(r):
-            for t in range(ROUND_TILES):
-                for h in range(N_HALVES):
-                    tile_index = r * ROUND_TILES + t
-                    n_cols = slice(h * N_HALF, (h + 1) * N_HALF)
-                    part = pre_act[tile_index][:, n_cols]
-                    nc.vector.tensor_tensor(out=part, in0=sums[(t, h)][:], in1=part, op=mybir.AluOpType.add)
-                    nc.scalar.activation(out=part, in_=part, func=mybir.ActivationFunctionType.Sigmoid)
-                    nc.sync.dma_start(out=out_rows[:, tile_index, n_cols], in_=part)
+        def finish(h):
+            n_cols = slice(h * N_HALF, (h + 1) * N_HALF)
+            for t in range(BATCH_TILES):
+                part = pre_act[t][:, n_cols]
+                nc.vector.tensor_tensor(out=part, in0=sums[(h, t)][:], in1=part, op=mybir.AluOpType.add)
+                nc.scalar.activation(out=part, in_=part, func=mybir.ActivationFunctionType.Sigmoid)
+                nc.sync.dma_start(out=out_rows[:, t, n_cols], in_=part)
 
+        plain_products(0)
         sort_pairs(0)
         flip(0)
+        plain_products(1)
         sort_pairs(1)
         for step in range(len(steps)):
             quantise(step)
@@ -222,12 +241,12 @@ def tile_stackrnn_pa_k_kernel(
                 flip(step + 1)
             if step + 2 < len(steps):
                 sort_pairs(step + 2)
-            if step < BATCH_TILES:
-                nc.vector.tensor_tensor(
-                    out=pre_act[step][:], in0=pre_act[step][:], in1=bias_all[:], op=mybir.AluOpType.add
-                )
-            r, c = steps[step]
-            if c == 0 and r > 0:
-                finish(r - 1)
-            multiply(step)
-        finish(ROUNDS - 1)
+            multiply(step, 1, 0)
+
+        for step in range(len(steps)):
+            load_weights(step, 1)
+        add_biases()
+        finish(0)
+        for first_step in range(0, len(steps), ROUND1_STEPS):
+            multiply(first_step, ROUND1_STEPS, 1)
+        finish(1)

@@ -23,9 +23,10 @@ N_HALVES = HDIM // N_HALF
 STEP_PASSES = 2
 SCALE_ROWS = K_PASS // 32
 RAW_BUFS = 6
-ROUND1_STEPS = 3
-
-assert (IDIM + HDIM) // (K_PASS * STEP_PASSES) % ROUND1_STEPS == 0
+QUAD = 32
+QUADS = P // QUAD
+ROW_GROUPS = BATCH // QUAD
+VECTOR_STEPS = 2
 
 FLOPS = 2 * BATCH * HDIM * (IDIM + HDIM + 2 * SDIM)
 
@@ -42,8 +43,12 @@ def tile_stackrnn_pa_k_kernel(
             steps.append((source, first))
 
     activations = {
-        "x": x.rearrange("(p t) k -> p t k", t=BATCH_TILES),
-        "hidden": hidden.rearrange("(p t) k -> p t k", t=BATCH_TILES),
+        "x": x.rearrange("(t p) k -> p t k", p=P),
+        "hidden": hidden.rearrange("(t p) k -> p t k", p=P),
+    }
+    grouped_rows = {
+        "x": x.rearrange("(r j) k -> j r k", j=QUAD),
+        "hidden": hidden.rearrange("(r j) k -> j r k", j=QUAD),
     }
     word_rows = {
         "x": Wi_words.bitcast(I32).rearrange("g p m -> p g m"),
@@ -53,7 +58,12 @@ def tile_stackrnn_pa_k_kernel(
         "x": Wi_scales.bitcast(I32).rearrange("g (two i) n -> i two g n", two=2),
         "hidden": Wh_scales.bitcast(I32).rearrange("g (two i) n -> i two g n", two=2),
     }
-    out_rows = out.rearrange("(p t) n -> p t n", t=BATCH_TILES)
+    out_rows = out.rearrange("(t p) n -> p t n", p=P)
+    tensor_steps = len(steps) - VECTOR_STEPS
+    vector_passes = []
+    for step in range(tensor_steps, len(steps)):
+        for g in range(STEP_PASSES):
+            vector_passes.append((step, g))
 
     with ExitStack() as ctx:
         keep = ctx.enter_context(tc.tile_pool(name="keep", bufs=1))
@@ -78,6 +88,7 @@ def tile_stackrnn_pa_k_kernel(
                 nc.vector.memset(w_planes[(source, h)][:].bitcast(I32), 0)
 
         raw_tiles = {}
+        vector_raw = {}
         w_words = {}
 
         def load_activations(step):
@@ -104,19 +115,58 @@ def tile_stackrnn_pa_k_kernel(
             )
             w_words[(h, step)] = words
 
-        def fetch(k):
-            if 0 <= k - 2 < len(steps):
-                load_weights(k - 2, 0)
-            if k < len(steps):
-                load_activations(k)
+        def load_quadrants(v):
+            step, g = vector_passes[v]
+            source, first = steps[step]
+            raw = raw_pool.tile([P, ROW_GROUPS, K_PASS // QUADS], BF16, name="raw")
+            for c in range(QUADS):
+                k_first = (first + g) * K_PASS + c * (K_PASS // QUADS)
+                nc.sync.dma_start(
+                    out=raw[c * QUAD : (c + 1) * QUAD, :, :],
+                    in_=grouped_rows[source][:, :, k_first : k_first + K_PASS // QUADS],
+                )
+            vector_raw[v] = raw
+
+        load_plan = []
+        for k in range(tensor_steps + 2):
+            if 0 <= k - 2:
+                load_plan.append(("weights", k - 2, 0))
+            if k < tensor_steps:
+                load_plan.append(("rows", k, 0))
+        for step in range(tensor_steps, len(steps)):
+            load_plan.append(("weights", step, 0))
+        for step in range(tensor_steps):
+            load_plan.append(("weights", step, 1))
+        for v in range(len(vector_passes)):
+            load_plan.append(("quadrants", v, 0))
+        for step in range(tensor_steps, len(steps)):
+            load_plan.append(("weights", step, 1))
+        progress = {"issued": 0, "free_raw": RAW_BUFS}
+
+        def issue_loads():
+            for kind, index, h in load_plan[progress["issued"] :]:
+                if kind != "weights":
+                    if progress["free_raw"] == 0:
+                        return
+                    progress["free_raw"] -= 1
+                progress["issued"] += 1
+                if kind == "weights":
+                    load_weights(index, h)
+                elif kind == "rows":
+                    load_activations(index)
+                else:
+                    load_quadrants(index)
+
+        def raw_tile_read():
+            progress["free_raw"] += 1
+            issue_loads()
 
         st_raw = keep.tile([P, BATCH_TILES, 2 * SDIM], BF16)
-        nc.sync.dma_start(out=st_raw[:], in_=stack_top.rearrange("(p t) j s -> p t (j s)", t=BATCH_TILES))
+        nc.sync.dma_start(out=st_raw[:], in_=stack_top.rearrange("(t p) j s -> p t (j s)", p=P))
         ws_raw = keep.tile([P, HDIM // P, 2, SDIM], BF16)
         for j, w_stack in enumerate((W0, W1)):
             nc.sync.dma_start(out=ws_raw[:, :, j, :], in_=w_stack.rearrange("(c p) s -> p c s", p=P))
-        for k in range(RAW_BUFS):
-            fetch(k)
+        issue_loads()
         for row, bias in enumerate((bi, bh, b0, b1)):
             nc.sync.dma_start(out=bias_rows[row : row + 1, :], in_=bias.rearrange("(o n) -> o n", o=1))
 
@@ -125,8 +175,8 @@ def tile_stackrnn_pa_k_kernel(
             nc.tensor.transpose(st_flipped[:, t, :], st_raw[:, t, :].bitcast(F32), ident[:])
         st_T = keep.tile([P, BATCH_TILES, P, 2], BF16)
         nc.vector.tensor_copy(
-            out=st_T[:].rearrange("q t b e -> q (t b e)"),
-            in_=st_flipped[:].rearrange("q t b -> q (t b)").bitcast(BF16),
+            out=st_T[:].rearrange("q t b e -> q (t b e)").bitcast(F32),
+            in_=st_flipped[:].rearrange("q t b -> q (t b)"),
         )
         ws_T = []
         blocks = N_HALF // P
@@ -140,8 +190,8 @@ def tile_stackrnn_pa_k_kernel(
                 )
             ws_T.append(keep.tile([P, N_HALF, 2], BF16, name="ws_T_%d" % h))
             nc.scalar.copy(
-                out=ws_T[h][:].rearrange("q n e -> q (n e)"),
-                in_=ws_flipped[:].rearrange("q c n -> q (c n)").bitcast(BF16),
+                out=ws_T[h][:].rearrange("q n e -> q (n e)").bitcast(F32),
+                in_=ws_flipped[:].rearrange("q c n -> q (c n)"),
             )
 
         pre_act = []
@@ -170,16 +220,17 @@ def tile_stackrnn_pa_k_kernel(
         sorted_tiles = {}
         grouped_tiles = {}
         code_tiles = {}
+        vector_codes = {}
         sums = {}
 
         def sort_pairs(step):
-            sorted_pairs = stage.tile([P, BATCH_TILES, STEP_PASSES, PAIRS, P], F32, name="sorted_pairs")
+            sorted_pairs = stage.tile([P, BATCH_TILES, STEP_PASSES, PAIRS, P], F32, name="sorted_pairs", align_bytes=64)
             nc.vector.tensor_copy(
                 out=sorted_pairs[:],
                 in_=raw_tiles[step][:].bitcast(F32).rearrange("p t (g q u) -> p t g u q", q=P, u=PAIRS),
             )
             sorted_tiles[step] = sorted_pairs
-            fetch(step + RAW_BUFS)
+            raw_tile_read()
 
         def flip(step):
             grouped = stage.tile([P, BATCH_TILES * STEP_PASSES * P * PACK], BF16, name="grouped", align_bytes=64)
@@ -200,53 +251,75 @@ def tile_stackrnn_pa_k_kernel(
             nc.vector.quantize_mx(out=codes[:].bitcast(FP8X4), scales=x_planes[:], in_=grouped_tiles[step][:])
             code_tiles[step] = (codes, x_planes)
 
-        def multiply(first_step, n_steps, h):
+        def turn(v):
+            sorted_pairs = stage.tile([P, ROW_GROUPS, PAIRS, QUAD], F32, name="sorted_pairs", align_bytes=64)
+            nc.scalar.copy(
+                out=sorted_pairs[:], in_=vector_raw[v][:].bitcast(F32).rearrange("p r (i u) -> p r u i", u=PAIRS)
+            )
+            raw_tile_read()
+            turned = stage.tile([P, ROW_GROUPS * PAIRS * QUAD], F32, name="turned", align_bytes=64)
+            nc.vector.transpose(out=turned[:], in_=sorted_pairs[:].rearrange("p r u i -> p (r u i)"))
+            grouped = stage.tile([P, BATCH * PACK], BF16, name="grouped", align_bytes=64)
+            nc.vector.tensor_copy(
+                out=grouped[:].bitcast(F32).rearrange("q (r j u) -> q r j u", j=QUAD, u=PAIRS),
+                in_=turned[:].rearrange("q (r u j) -> q r j u", u=PAIRS, j=QUAD),
+            )
+            codes = keep.tile([P, BATCH], U32, name="vector_codes_%d" % v, align_bytes=64)
+            x_planes = keep.tile([P, BATCH], U8, name="vector_planes_%d" % v, align_bytes=64)
+            nc.vector.quantize_mx(out=codes[:].bitcast(FP8X4), scales=x_planes[:], in_=grouped[:])
+            vector_codes[v] = (codes, x_planes)
+
+        def one_pass(h, t, step, g, operand, first_column, start, stop):
+            source, first = steps[step]
+            codes, x_planes = operand
+            b_cols = slice(first_column, first_column + P)
+            nc.tensor.matmul_mx(
+                out=sums[(h, t)][:],
+                lhsT=codes[:, b_cols].bitcast(FP8X4),
+                lhsT_scale=x_planes[:, b_cols],
+                rhs=w_words[(h, step)][:, g, :].bitcast(FP4X4),
+                rhs_scale=w_planes[(source, h)][:, first + g, :],
+                start=start,
+                stop=stop,
+            )
+
+        def multiply(step, h):
             for t in range(BATCH_TILES):
-                if first_step == 0:
+                if step == 0:
                     if h == 0:
                         sums[(h, t)] = sums_pool.tile([P, N_HALF], F32, name="sums", tag="sums")
                     else:
                         sums[(h, t)] = work.tile([P, N_HALF], F32, name="sums", tag="work")
-                for step in range(first_step, first_step + n_steps):
-                    source, first = steps[step]
-                    codes, x_planes = code_tiles[step]
-                    for g in range(STEP_PASSES):
-                        b_cols = slice((t * STEP_PASSES + g) * P, (t * STEP_PASSES + g + 1) * P)
-                        nc.tensor.matmul_mx(
-                            out=sums[(h, t)][:],
-                            lhsT=codes[:, b_cols].bitcast(FP8X4),
-                            lhsT_scale=x_planes[:, b_cols],
-                            rhs=w_words[(h, step)][:, g, :].bitcast(FP4X4),
-                            rhs_scale=w_planes[(source, h)][:, first + g, :],
-                            start=(step == 0 and g == 0),
-                            stop=(step == len(steps) - 1 and g == STEP_PASSES - 1),
-                        )
+                for g in range(STEP_PASSES):
+                    one_pass(h, t, step, g, code_tiles[step], (t * STEP_PASSES + g) * P, step == 0 and g == 0, False)
 
-        def finish(h):
-            n_cols = slice(h * N_HALF, (h + 1) * N_HALF)
-            for t in range(BATCH_TILES):
-                part = pre_act[t][:, n_cols]
-                nc.vector.tensor_tensor(out=part, in0=sums[(h, t)][:], in1=part, op=mybir.AluOpType.add)
-                nc.scalar.activation(out=part, in_=part, func=mybir.ActivationFunctionType.Sigmoid)
-                nc.sync.dma_start(out=out_rows[:, t, n_cols], in_=part)
+        def close(h, t):
+            for v in range(len(vector_passes)):
+                step, g = vector_passes[v]
+                one_pass(h, t, step, g, vector_codes[v], t * P, False, v == len(vector_passes) - 1)
+            part = pre_act[t][:, h * N_HALF : (h + 1) * N_HALF]
+            nc.vector.tensor_tensor(out=part, in0=sums[(h, t)][:], in1=part, op=mybir.AluOpType.add)
+            nc.scalar.activation(out=part, in_=part, func=mybir.ActivationFunctionType.Sigmoid)
+            nc.sync.dma_start(out=out_rows[:, t, h * N_HALF : (h + 1) * N_HALF], in_=part)
 
         plain_products(0)
         sort_pairs(0)
         flip(0)
         plain_products(1)
         sort_pairs(1)
-        for step in range(len(steps)):
+        for step in range(tensor_steps):
             quantise(step)
-            if step + 1 < len(steps):
+            if step + 1 < tensor_steps:
                 flip(step + 1)
-            if step + 2 < len(steps):
+            if step + 2 < tensor_steps:
                 sort_pairs(step + 2)
-            multiply(step, 1, 0)
+            multiply(step, 0)
 
-        for step in range(len(steps)):
-            load_weights(step, 1)
         add_biases()
-        finish(0)
-        for first_step in range(0, len(steps), ROUND1_STEPS):
-            multiply(first_step, ROUND1_STEPS, 1)
-        finish(1)
+        for v in range(len(vector_passes)):
+            turn(v)
+        for step in range(tensor_steps):
+            multiply(step, 1)
+        for h in range(N_HALVES):
+            for t in range(BATCH_TILES):
+                close(h, t)

@@ -27,6 +27,7 @@ QUAD = 32
 QUADS = P // QUAD
 ROW_GROUPS = BATCH // QUAD
 VECTOR_STEPS = 2
+CLOSING_PASSES = 2
 
 FLOPS = 2 * BATCH * HDIM * (IDIM + HDIM + 2 * SDIM)
 
@@ -133,14 +134,16 @@ def tile_stackrnn_pa_k_kernel(
                 load_plan.append(("weights", k - 2, 0))
             if k < tensor_steps:
                 load_plan.append(("rows", k, 0))
-        for step in range(tensor_steps, len(steps)):
-            load_plan.append(("weights", step, 0))
+        late_weights = []
         for step in range(tensor_steps):
-            load_plan.append(("weights", step, 1))
-        for v in range(len(vector_passes)):
-            load_plan.append(("quadrants", v, 0))
+            late_weights.append(("weights", step, 1))
         for step in range(tensor_steps, len(steps)):
-            load_plan.append(("weights", step, 1))
+            for h in range(N_HALVES):
+                late_weights.append(("weights", step, h))
+        for place, load in enumerate(late_weights):
+            load_plan.append(load)
+            if place % 2 == 1 and place // 2 < len(vector_passes):
+                load_plan.append(("quadrants", place // 2, 0))
         progress = {"issued": 0, "free_raw": RAW_BUFS}
 
         def issue_loads():
@@ -293,10 +296,13 @@ def tile_stackrnn_pa_k_kernel(
                 for g in range(STEP_PASSES):
                     one_pass(h, t, step, g, code_tiles[step], (t * STEP_PASSES + g) * P, step == 0 and g == 0, False)
 
+        def vector_pass(h, t, v):
+            step, g = vector_passes[v]
+            one_pass(h, t, step, g, vector_codes[v], t * P, False, v == len(vector_passes) - 1)
+
         def close(h, t):
-            for v in range(len(vector_passes)):
-                step, g = vector_passes[v]
-                one_pass(h, t, step, g, vector_codes[v], t * P, False, v == len(vector_passes) - 1)
+            for v in range(len(vector_passes) - CLOSING_PASSES, len(vector_passes)):
+                vector_pass(h, t, v)
             part = pre_act[t][:, h * N_HALF : (h + 1) * N_HALF]
             nc.vector.tensor_tensor(out=part, in0=sums[(h, t)][:], in1=part, op=mybir.AluOpType.add)
             nc.scalar.activation(out=part, in_=part, func=mybir.ActivationFunctionType.Sigmoid)
@@ -320,6 +326,10 @@ def tile_stackrnn_pa_k_kernel(
             turn(v)
         for step in range(tensor_steps):
             multiply(step, 1)
+        for v in range(len(vector_passes) - CLOSING_PASSES):
+            for h in range(N_HALVES):
+                for t in range(BATCH_TILES):
+                    vector_pass(h, t, v)
         for h in range(N_HALVES):
             for t in range(BATCH_TILES):
                 close(h, t)

@@ -84,7 +84,7 @@ def tile_stackrnn_pa_k_kernel(
         for h in range(N_HALVES):
             for source in ("x", "hidden"):
                 w_planes[(source, h)] = keep.tile(
-                    [P, k_sizes[source] // K_PASS, N_HALF], U8, name="w_planes_%s_%d" % (source, h), align_bytes=64
+                    [P, k_sizes[source] // K_PASS, N_HALF], U8, name="w_planes_%s_%d" % (source, h), align_bytes=256
                 )
                 nc.vector.memset(w_planes[(source, h)][:].bitcast(I32), 0)
 
@@ -109,7 +109,7 @@ def tile_stackrnn_pa_k_kernel(
                         out=w_planes[(source, h)][partition:P:64, :, :].bitcast(I32),
                         in_=scale_rows[source][i, :, :, h * N_HALF // 4 : (h + 1) * N_HALF // 4],
                     )
-            words = keep.tile([P, STEP_PASSES, 2 * N_HALF], U8, name="w_words_%d_%d" % (h, step), align_bytes=64)
+            words = keep.tile([P, STEP_PASSES, 2 * N_HALF], U8, name="w_words_%d_%d" % (h, step), align_bytes=256)
             nc.sync.dma_start(
                 out=words[:].bitcast(I32),
                 in_=word_rows[source][:, first : first + STEP_PASSES, h * N_HALF // 2 : (h + 1) * N_HALF // 2],
@@ -249,8 +249,8 @@ def tile_stackrnn_pa_k_kernel(
             grouped_tiles[step] = grouped
 
         def quantise(step):
-            codes = keep.tile([P, BATCH_TILES * STEP_PASSES * P], U32, name="codes_%d" % step, align_bytes=64)
-            x_planes = keep.tile([P, BATCH_TILES * STEP_PASSES * P], U8, name="x_planes_%d" % step, align_bytes=64)
+            codes = keep.tile([P, BATCH_TILES * STEP_PASSES * P], U32, name="codes_%d" % step, align_bytes=256)
+            x_planes = keep.tile([P, BATCH_TILES * STEP_PASSES * P], U8, name="x_planes_%d" % step, align_bytes=256)
             nc.vector.quantize_mx(out=codes[:].bitcast(FP8X4), scales=x_planes[:], in_=grouped_tiles[step][:])
             code_tiles[step] = (codes, x_planes)
 
@@ -267,8 +267,8 @@ def tile_stackrnn_pa_k_kernel(
                 out=grouped[:].bitcast(F32).rearrange("q (r j u) -> q r j u", j=QUAD, u=PAIRS),
                 in_=turned[:].rearrange("q (r u j) -> q r j u", u=PAIRS, j=QUAD),
             )
-            codes = keep.tile([P, BATCH], U32, name="vector_codes_%d" % v, align_bytes=64)
-            x_planes = keep.tile([P, BATCH], U8, name="vector_planes_%d" % v, align_bytes=64)
+            codes = keep.tile([P, BATCH], U32, name="vector_codes_%d" % v, align_bytes=256)
+            x_planes = keep.tile([P, BATCH], U8, name="vector_planes_%d" % v, align_bytes=256)
             nc.vector.quantize_mx(out=codes[:].bitcast(FP8X4), scales=x_planes[:], in_=grouped[:])
             vector_codes[v] = (codes, x_planes)
 

@@ -100,15 +100,16 @@ def tile_stackrnn_pa_k_kernel(
             )
             raw_tiles[step] = raw
 
+        def load_scales(source, h):
+            for i in range(SCALE_ROWS // 2):
+                partition = 32 * (i // 4) + i % 4
+                nc.sync.dma_start(
+                    out=w_planes[(source, h)][partition:P:64, :, :].bitcast(I32),
+                    in_=scale_rows[source][i, :, :, h * N_HALF // 4 : (h + 1) * N_HALF // 4],
+                )
+
         def load_weights(step, h):
             source, first = steps[step]
-            if first == 0:
-                for i in range(SCALE_ROWS // 2):
-                    partition = 32 * (i // 4) + i % 4
-                    nc.sync.dma_start(
-                        out=w_planes[(source, h)][partition:P:64, :, :].bitcast(I32),
-                        in_=scale_rows[source][i, :, :, h * N_HALF // 4 : (h + 1) * N_HALF // 4],
-                    )
             words = keep.tile([P, STEP_PASSES, 2 * N_HALF], U8, name="w_words_%d_%d" % (h, step), align_bytes=256)
             nc.sync.dma_start(
                 out=words[:].bitcast(I32),
@@ -130,10 +131,15 @@ def tile_stackrnn_pa_k_kernel(
 
         load_plan = []
         for k in range(tensor_steps + 2):
+            if k - 2 == 0:
+                load_plan.append(("scales", "x", 0))
             if 0 <= k - 2:
                 load_plan.append(("weights", k - 2, 0))
             if k < tensor_steps:
                 load_plan.append(("rows", k, 0))
+        load_plan.append(("scales", "x", 1))
+        for h in range(N_HALVES):
+            load_plan.append(("scales", "hidden", h))
         late_weights = []
         for step in range(tensor_steps):
             late_weights.append(("weights", step, 1))
@@ -148,13 +154,15 @@ def tile_stackrnn_pa_k_kernel(
 
         def issue_loads():
             for kind, index, h in load_plan[progress["issued"] :]:
-                if kind != "weights":
+                if kind in ("rows", "quadrants"):
                     if progress["free_raw"] == 0:
                         return
                     progress["free_raw"] -= 1
                 progress["issued"] += 1
                 if kind == "weights":
                     load_weights(index, h)
+                elif kind == "scales":
+                    load_scales(index, h)
                 elif kind == "rows":
                     load_activations(index)
                 else:

@@ -28,6 +28,7 @@ QUADS = P // QUAD
 ROW_GROUPS = BATCH // QUAD
 VECTOR_STEPS = 2
 CLOSING_PASSES = 2
+QUANTISE_CALLS = 4
 
 FLOPS = 2 * BATCH * HDIM * (IDIM + HDIM + 2 * SDIM)
 
@@ -259,7 +260,13 @@ def tile_stackrnn_pa_k_kernel(
         def quantise(step):
             codes = keep.tile([P, BATCH_TILES * STEP_PASSES * P], U32, name="codes_%d" % step, align_bytes=256)
             x_planes = keep.tile([P, BATCH_TILES * STEP_PASSES * P], U8, name="x_planes_%d" % step, align_bytes=256)
-            nc.vector.quantize_mx(out=codes[:].bitcast(FP8X4), scales=x_planes[:], in_=grouped_tiles[step][:])
+            columns = BATCH_TILES * STEP_PASSES * P // QUANTISE_CALLS
+            for call in range(QUANTISE_CALLS):
+                nc.vector.quantize_mx(
+                    out=codes[:, call * columns : (call + 1) * columns].bitcast(FP8X4),
+                    scales=x_planes[:, call * columns : (call + 1) * columns],
+                    in_=grouped_tiles[step][:, call * columns * PACK : (call + 1) * columns * PACK],
+                )
             code_tiles[step] = (codes, x_planes)
 
         def turn(v):

from contextlib import ExitStack

import concourse.mybir as mybir
from concourse.masks import make_identity

F32 = mybir.dt.float32
BF16 = mybir.dt.bfloat16
I32 = mybir.dt.int32
U32 = mybir.dt.uint32
U8 = mybir.dt.uint8
FP8X4 = mybir.dt.float8_e4m3fn_x4
FP4X4 = mybir.dt.float4_e2m1fn_x4

P = 128
PACK = 4
K_PASS = P * PACK
PAIRS = 2

BATCH, IDIM, HDIM, SDIM = 512, 8192, 1024, 128
BATCH_TILES = BATCH // P
N_HALF = 512
N_HALVES = HDIM // N_HALF
STEP_PASSES = 2
SCALE_ROWS = K_PASS // 32
RAW_BUFS = 6
QUAD = 32
QUADS = P // QUAD
ROW_GROUPS = BATCH // QUAD
VECTOR_STEPS = 2
CLOSING_PASSES = 2
QUANTISE_CALLS = 4

FLOPS = 2 * BATCH * HDIM * (IDIM + HDIM + 2 * SDIM)


def tile_stackrnn_pa_k_kernel(
    tc, x, hidden, stack_top, Wi_words, Wi_scales, bi, Wh_words, Wh_scales, bh, W0, b0, W1, b1, out
):
    nc = tc.nc

    k_sizes = {"x": IDIM, "hidden": HDIM}
    steps = []
    for source in ("x", "hidden"):
        for first in range(0, k_sizes[source] // K_PASS, STEP_PASSES):
            steps.append((source, first))

    activations = {
        "x": x.rearrange("(t p) k -> p t k", p=P),
        "hidden": hidden.rearrange("(t p) k -> p t k", p=P),
    }
    grouped_rows = {
        "x": x.rearrange("(r j) k -> j r k", j=QUAD),
        "hidden": hidden.rearrange("(r j) k -> j r k", j=QUAD),
    }
    word_rows = {
        "x": Wi_words.bitcast(I32).rearrange("g p m -> p g m"),
        "hidden": Wh_words.bitcast(I32).rearrange("g p m -> p g m"),
    }
    scale_rows = {
        "x": Wi_scales.bitcast(I32).rearrange("g (two i) n -> i two g n", two=2),
        "hidden": Wh_scales.bitcast(I32).rearrange("g (two i) n -> i two g n", two=2),
    }
    out_rows = out.rearrange("(t p) n -> p t n", p=P)
    tensor_steps = len(steps) - VECTOR_STEPS
    vector_passes = []
    for step in range(tensor_steps, len(steps)):
        for g in range(STEP_PASSES):
            vector_passes.append((step, g))

    with ExitStack() as ctx:
        keep = ctx.enter_context(tc.tile_pool(name="keep", bufs=1))
        raw_pool = ctx.enter_context(tc.tile_pool(name="raw_pool", bufs=RAW_BUFS))
        stage = ctx.enter_context(tc.tile_pool(name="stage", bufs=2))
        sums_pool = ctx.enter_context(tc.psum_pool(name="sums_pool", bufs=BATCH_TILES))
        work = ctx.enter_context(tc.psum_pool(name="work", bufs=4))
        ctx.enter_context(tc.manual_schedule())

        ident = keep.tile([P, P], F32)
        make_identity(nc, ident[:])
        ones = keep.tile([P, P], BF16)
        nc.vector.memset(ones[:], 1.0)
        bias_rows = keep.tile([P, HDIM], BF16)
        nc.vector.memset(bias_rows[:], 0.0)
        w_planes = {}
        for h in range(N_HALVES):
            for source in ("x", "hidden"):
                w_planes[(source, h)] = keep.tile(
                    [P, k_sizes[source] // K_PASS, N_HALF], U8, name="w_planes_%s_%d" % (source, h), align_bytes=256
                )
                nc.vector.memset(w_planes[(source, h)][:].bitcast(I32), 0)

        raw_tiles = {}
        vector_raw = {}
        w_words = {}

        def load_activations(step):
            source, first = steps[step]
            raw = raw_pool.tile([P, BATCH_TILES, STEP_PASSES * K_PASS], BF16, name="raw")
            nc.sync.dma_start(
                out=raw[:], in_=activations[source][:, :, first * K_PASS : (first + STEP_PASSES) * K_PASS]
            )
            raw_tiles[step] = raw

        def load_scales(source, h):
            for i in range(SCALE_ROWS // 2):
                partition = 32 * (i // 4) + i % 4
                nc.sync.dma_start(
                    out=w_planes[(source, h)][partition:P:64, :, :].bitcast(I32),
                    in_=scale_rows[source][i, :, :, h * N_HALF // 4 : (h + 1) * N_HALF // 4],
                )

        def load_weights(step, h):
            source, first = steps[step]
            words = keep.tile([P, STEP_PASSES, 2 * N_HALF], U8, name="w_words_%d_%d" % (h, step), align_bytes=256)
            nc.sync.dma_start(
                out=words[:].bitcast(I32),
                in_=word_rows[source][:, first : first + STEP_PASSES, h * N_HALF // 2 : (h + 1) * N_HALF // 2],
            )
            w_words[(h, step)] = words

        def load_quadrants(v):
            step, g = vector_passes[v]
            source, first = steps[step]
            raw = raw_pool.tile([P, ROW_GROUPS, K_PASS // QUADS], BF16, name="raw")
            for c in range(QUADS):
                k_first = (first + g) * K_PASS + c * (K_PASS // QUADS)
                nc.sync.dma_start(
                    out=raw[c * QUAD : (c + 1) * QUAD, :, :],
                    in_=grouped_rows[source][:, :, k_first : k_first + K_PASS // QUADS],
                )
            vector_raw[v] = raw

        load_plan = []
        for k in range(tensor_steps + 2):
            if k - 2 == 0:
                load_plan.append(("scales", "x", 0))
            if 0 <= k - 2:
                load_plan.append(("weights", k - 2, 0))
            if k < tensor_steps:
                load_plan.append(("rows", k, 0))
        load_plan.append(("scales", "x", 1))
        for h in range(N_HALVES):
            load_plan.append(("scales", "hidden", h))
        late_weights = []
        for step in range(tensor_steps):
            late_weights.append(("weights", step, 1))
        for step in range(tensor_steps, len(steps)):
            for h in range(N_HALVES):
                late_weights.append(("weights", step, h))
        for place, load in enumerate(late_weights):
            load_plan.append(load)
            if place % 2 == 1 and place // 2 < len(vector_passes):
                load_plan.append(("quadrants", place // 2, 0))
        progress = {"issued": 0, "free_raw": RAW_BUFS}

        def issue_loads():
            for kind, index, h in load_plan[progress["issued"] :]:
                if kind in ("rows", "quadrants"):
                    if progress["free_raw"] == 0:
                        return
                    progress["free_raw"] -= 1
                progress["issued"] += 1
                if kind == "weights":
                    load_weights(index, h)
                elif kind == "scales":
                    load_scales(index, h)
                elif kind == "rows":
                    load_activations(index)
                else:
                    load_quadrants(index)

        def raw_tile_read():
            progress["free_raw"] += 1
            issue_loads()

        st_raw = keep.tile([P, BATCH_TILES, 2 * SDIM], BF16)
        nc.sync.dma_start(out=st_raw[:], in_=stack_top.rearrange("(t p) j s -> p t (j s)", p=P))
        ws_raw = keep.tile([P, HDIM // P, 2, SDIM], BF16)
        for j, w_stack in enumerate((W0, W1)):
            nc.sync.dma_start(out=ws_raw[:, :, j, :], in_=w_stack.rearrange("(c p) s -> p c s", p=P))
        issue_loads()
        for row, bias in enumerate((bi, bh, b0, b1)):
            nc.sync.dma_start(out=bias_rows[row : row + 1, :], in_=bias.rearrange("(o n) -> o n", o=1))

        st_flipped = work.tile([P, BATCH_TILES, P], F32, tag="work")
        for t in range(BATCH_TILES):
            nc.tensor.transpose(st_flipped[:, t, :], st_raw[:, t, :].bitcast(F32), ident[:])
        st_T = keep.tile([P, BATCH_TILES, P, 2], BF16)
        nc.vector.tensor_copy(
            out=st_T[:].rearrange("q t b e -> q (t b e)").bitcast(F32),
            in_=st_flipped[:].rearrange("q t b -> q (t b)"),
        )
        ws_T = []
        blocks = N_HALF // P
        for h in range(N_HALVES):
            ws_flipped = work.tile([P, blocks, P], F32, tag="work")
            for c in range(blocks):
                nc.tensor.transpose(
                    ws_flipped[:, c, :],
                    ws_raw[:, h * blocks + c, :, :].rearrange("p j s -> p (j s)").bitcast(F32),
                    ident[:],
                )
            ws_T.append(keep.tile([P, N_HALF, 2], BF16, name="ws_T_%d" % h))
            nc.scalar.copy(
                out=ws_T[h][:].rearrange("q n e -> q (n e)").bitcast(F32),
                in_=ws_flipped[:].rearrange("q c n -> q (c n)"),
            )

        pre_act = []
        for t in range(BATCH_TILES):
            pre_act.append(keep.tile([P, HDIM], F32, name="pre_act_%d" % t))

        def plain_products(h):
            for t in range(BATCH_TILES):
                plain = sums_pool.tile([P, N_HALF], F32, tag="sums")
                for e in range(2):
                    nc.tensor.matmul(
                        out=plain[:], lhsT=st_T[:, t, :, e], rhs=ws_T[h][:, :, e], start=(e == 0), stop=(e == 1)
                    )
                nc.scalar.copy(out=pre_act[t][:, h * N_HALF : (h + 1) * N_HALF], in_=plain[:])

        def add_biases():
            bias_all = keep.tile([P, HDIM], F32)
            for h in range(N_HALVES):
                n_cols = slice(h * N_HALF, (h + 1) * N_HALF)
                spread = work.tile([P, N_HALF], F32, tag="work")
                nc.tensor.matmul(out=spread[:], lhsT=ones[:], rhs=bias_rows[:, n_cols], start=True, stop=True)
                nc.scalar.copy(out=bias_all[:, n_cols], in_=spread[:])
            for t in range(BATCH_TILES):
                nc.vector.tensor_tensor(out=pre_act[t][:], in0=pre_act[t][:], in1=bias_all[:], op=mybir.AluOpType.add)

        sorted_tiles = {}
        grouped_tiles = {}
        code_tiles = {}
        vector_codes = {}
        sums = {}

        def sort_pairs(step):
            sorted_pairs = stage.tile([P, BATCH_TILES, STEP_PASSES, PAIRS, P], F32, name="sorted_pairs", align_bytes=64)
            nc.vector.tensor_copy(
                out=sorted_pairs[:],
                in_=raw_tiles[step][:].bitcast(F32).rearrange("p t (g q u) -> p t g u q", q=P, u=PAIRS),
            )
            sorted_tiles[step] = sorted_pairs
            raw_tile_read()

        def flip(step):
            grouped = stage.tile([P, BATCH_TILES * STEP_PASSES * P * PACK], BF16, name="grouped", align_bytes=64)
            grouped_pairs = grouped[:].bitcast(F32).rearrange(
                "q (t g b u) -> q t g b u", t=BATCH_TILES, g=STEP_PASSES, u=PAIRS
            )
            for t in range(BATCH_TILES):
                flipped = work.tile([P, STEP_PASSES, PAIRS, P], F32, tag="work")
                for g in range(STEP_PASSES):
                    for u in range(PAIRS):
                        nc.tensor.transpose(flipped[:, g, u, :], sorted_tiles[step][:, t, g, u, :], ident[:])
                nc.scalar.copy(out=grouped_pairs[:, t], in_=flipped[:].rearrange("q g u b -> q g b u"))
            grouped_tiles[step] = grouped

        def quantise(step):
            codes = keep.tile([P, BATCH_TILES * STEP_PASSES * P], U32, name="codes_%d" % step, align_bytes=256)
            x_planes = keep.tile([P, BATCH_TILES * STEP_PASSES * P], U8, name="x_planes_%d" % step, align_bytes=256)
            columns = BATCH_TILES * STEP_PASSES * P // QUANTISE_CALLS
            for call in range(QUANTISE_CALLS):
                nc.vector.quantize_mx(
                    out=codes[:, call * columns : (call + 1) * columns].bitcast(FP8X4),
                    scales=x_planes[:, call * columns : (call + 1) * columns],
                    in_=grouped_tiles[step][:, call * columns * PACK : (call + 1) * columns * PACK],
                )
            code_tiles[step] = (codes, x_planes)

        def turn(v):
            sorted_pairs = stage.tile([P, ROW_GROUPS, PAIRS, QUAD], F32, name="sorted_pairs", align_bytes=64)
            nc.scalar.copy(
                out=sorted_pairs[:], in_=vector_raw[v][:].bitcast(F32).rearrange("p r (i u) -> p r u i", u=PAIRS)
            )
            raw_tile_read()
            turned = stage.tile([P, ROW_GROUPS * PAIRS * QUAD], F32, name="turned", align_bytes=64)
            nc.vector.transpose(out=turned[:], in_=sorted_pairs[:].rearrange("p r u i -> p (r u i)"))
            grouped = stage.tile([P, BATCH * PACK], BF16, name="grouped", align_bytes=64)
            nc.vector.tensor_copy(
                out=grouped[:].bitcast(F32).rearrange("q (r j u) -> q r j u", j=QUAD, u=PAIRS),
                in_=turned[:].rearrange("q (r u j) -> q r j u", u=PAIRS, j=QUAD),
            )
            codes = keep.tile([P, BATCH], U32, name="vector_codes_%d" % v, align_bytes=256)
            x_planes = keep.tile([P, BATCH], U8, name="vector_planes_%d" % v, align_bytes=256)
            nc.vector.quantize_mx(out=codes[:].bitcast(FP8X4), scales=x_planes[:], in_=grouped[:])
            vector_codes[v] = (codes, x_planes)

        def one_pass(h, t, step, g, operand, first_column, start, stop):
            source, first = steps[step]
            codes, x_planes = operand
            b_cols = slice(first_column, first_column + P)
            nc.tensor.matmul_mx(
                out=sums[(h, t)][:],
                lhsT=codes[:, b_cols].bitcast(FP8X4),
                lhsT_scale=x_planes[:, b_cols],
                rhs=w_words[(h, step)][:, g, :].bitcast(FP4X4),
                rhs_scale=w_planes[(source, h)][:, first + g, :],
                start=start,
                stop=stop,
            )

        def multiply(step, h):
            for t in range(BATCH_TILES):
                if step == 0:
                    if h == 0:
                        sums[(h, t)] = sums_pool.tile([P, N_HALF], F32, name="sums", tag="sums")
                    else:
                        sums[(h, t)] = work.tile([P, N_HALF], F32, name="sums", tag="work")
                for g in range(STEP_PASSES):
                    one_pass(h, t, step, g, code_tiles[step], (t * STEP_PASSES + g) * P, step == 0 and g == 0, False)

        def vector_pass(h, t, v):
            step, g = vector_passes[v]
            one_pass(h, t, step, g, vector_codes[v], t * P, False, v == len(vector_passes) - 1)

        def close(h, t):
            for v in range(len(vector_passes) - CLOSING_PASSES, len(vector_passes)):
                vector_pass(h, t, v)
            part = pre_act[t][:, h * N_HALF : (h + 1) * N_HALF]
            nc.vector.tensor_tensor(out=part, in0=sums[(h, t)][:], in1=part, op=mybir.AluOpType.add)
            nc.scalar.activation(out=part, in_=part, func=mybir.ActivationFunctionType.Sigmoid)
            nc.sync.dma_start(out=out_rows[:, t, h * N_HALF : (h + 1) * N_HALF], in_=part)

        plain_products(0)
        sort_pairs(0)
        flip(0)
        plain_products(1)
        sort_pairs(1)
        for step in range(tensor_steps):
            quantise(step)
            if step + 1 < tensor_steps:
                flip(step + 1)
            if step + 2 < tensor_steps:
                sort_pairs(step + 2)
            multiply(step, 0)

        add_biases()
        for v in range(len(vector_passes)):
            turn(v)
        for step in range(tensor_steps):
            multiply(step, 1)
        for v in range(len(vector_passes) - CLOSING_PASSES):
            for h in range(N_HALVES):
                for t in range(BATCH_TILES):
                    vector_pass(h, t, v)
        for h in range(N_HALVES):
            for t in range(BATCH_TILES):
                close(h, t)
